import numpy as np
import ml_dtypes


def mxq(x, axis, fmt="e4m3"):
    dtype, down = {"e4m3": (ml_dtypes.float8_e4m3fn, 7), "e5m2": (ml_dtypes.float8_e5m2, 14)}[fmt]
    v = np.moveaxis(np.asarray(x, np.float32).astype(ml_dtypes.bfloat16).astype(np.float64), axis, -1)
    blocks = v.reshape(v.shape[:-1] + (-1, 32))
    amax = np.abs(blocks).max(-1, keepdims=True)
    byte = np.maximum(np.where(amax > 0, np.frexp(amax)[1] - 1 + 127, 0) - down, 1)
    scale = np.exp2(byte - 127.0)
    codes = (blocks / scale).astype(np.float32).astype(dtype).astype(np.float64)
    return np.moveaxis((codes * scale).reshape(v.shape), -1, axis)


WIDE = False


def mx_kscale(k):
    if not WIDE:
        return np.ones(k)
    levels = np.array([10, -10, 5, -5, 0])
    a = np.random.permutation(np.resize(levels, k // 512 * 4)).reshape(k // 512, 4)
    idx = np.arange(k)
    return np.exp2(a[idx // 512, idx % 128 // 32])


BF16 = ml_dtypes.bfloat16


def bf(x):
    return np.asarray(x, np.float32).astype(BF16)


def f64(x):
    return np.asarray(x).astype(np.float64)


B, N, D, H = 3, 512, 512, 2048


def setup_inputs():
    s = mx_kscale(D)
    return {"xwx": bf(np.abs(np.random.standard_normal((B, N, N))) * 2.0),
            "inp": bf(np.random.standard_normal((B, N, D)) / np.sqrt(N) * s),
            "V": bf(np.random.standard_normal((D, D)) * 1.5 * np.sqrt(N / D) / s[None, :]),
            "x": bf(np.random.standard_normal((B, N, D)))}


def reference(xwx, inp, V, x):
    u = mxq(f64(V), 1, "e4m3") @ mxq(f64(inp), 2, "e4m3").transpose(0, 2, 1)
    vx = np.sqrt(np.square(u) + 1e-8)
    sc = f64(xwx)
    e = np.exp(sc - sc.max(-1, keepdims=True))
    t = (mxq(e, 2, "e4m3") @ mxq(vx, 2, "e4m3").transpose(0, 2, 1)) / e.sum(-1, keepdims=True)
    return f64(x) + t

@@ -1,0 +1,214 @@
+from contextlib import ExitStack
+
+import concourse.mybir as mybir
+from concourse.masks import make_identity
+
+F32 = mybir.dt.float32
+BF16 = mybir.dt.bfloat16
+U32 = mybir.dt.uint32
+U8 = mybir.dt.uint8
+FP8X4 = mybir.dt.float8_e4m3fn_x4
+ACT = mybir.ActivationFunctionType
+ALU = mybir.AluOpType
+AXIS = mybir.AxisListType
+
+P = 128
+PACK = 4
+IMAGES = 3
+SIZE = 512
+TILES = SIZE // P
+WORDS = SIZE // 2
+EPS = 1e-8
+
+FLOPS = 2 * 2 * IMAGES * SIZE * SIZE * SIZE
+
+
+def k_to_partitions(nc, psum, rows, identity, grouped):
+    row_words = rows.bitcast(F32)
+    grouped_words = grouped.bitcast(F32).rearrange(
+        "w (tile r half) -> w tile r half", tile=TILES, half=2
+    )
+    for pair in range(TILES // 2):
+        bank = psum.tile([P, 2, 2, P], F32, name="transposed")
+        for tile_in_pair in range(2):
+            for half in range(2):
+                nc.tensor.transpose(
+                    bank[:, tile_in_pair, half, :],
+                    row_words[:, 2 * pair + tile_in_pair, half * P : (half + 1) * P],
+                    identity,
+                )
+        nc.vector.tensor_copy(
+            out=grouped_words[:, 2 * pair : 2 * pair + 2, :, :],
+            in_=bank[:].rearrange("w tile half r -> w tile r half"),
+        )
+
+
+def quantise(nc, pool, grouped, name):
+    codes = pool.tile([P, SIZE], U32, name=name + "_codes", align_bytes=64)
+    scales = pool.tile([P, SIZE], U8, name=name + "_scales", align_bytes=64)
+    nc.vector.quantize_mx(out=codes[:].bitcast(FP8X4), scales=scales[:], in_=grouped)
+    return codes, scales
+
+
+def tile_quantumattentionblock_pb_kernel(tc, xwx, inp, V, x, out):
+    nc = tc.nc
+    with ExitStack() as ctx:
+        const = ctx.enter_context(tc.tile_pool(name="const", bufs=1))
+        sbuf = ctx.enter_context(tc.tile_pool(name="sbuf", bufs=IMAGES))
+        halves = ctx.enter_context(tc.tile_pool(name="halves", bufs=2 * IMAGES))
+        psum_transposed = ctx.enter_context(tc.psum_pool(name="psum_transposed", bufs=2))
+        psum_u = ctx.enter_context(tc.psum_pool(name="psum_u", bufs=3))
+        psum_t = ctx.enter_context(tc.psum_pool(name="psum_t", bufs=3))
+
+        identity = const.tile([P, P], F32, name="identity")
+        make_identity(nc, identity[:])
+        eps = const.tile([P, 1], F32, name="eps")
+        nc.vector.memset(eps[:], EPS)
+
+        xwx_sb = []
+        for b in range(IMAGES):
+            xwx_b = sbuf.tile([P, TILES, SIZE], BF16, name="xwx_sb")
+            xwx_rows = xwx[b].rearrange("(p j) n -> p j n", j=TILES)
+            for h in range(2):
+                nc.sync.dma_start(
+                    out=xwx_b[:, 2 * h : 2 * h + 2, :], in_=xwx_rows[:, 2 * h : 2 * h + 2, :]
+                )
+            xwx_sb.append(xwx_b)
+        v_sb = const.tile([P, TILES, SIZE], BF16, name="v_sb")
+        nc.sync.dma_start(out=v_sb[:], in_=V.rearrange("(r p) f -> p r f", p=P))
+        inp_sb = []
+        for b in range(IMAGES):
+            inp_b = sbuf.tile([P, TILES, SIZE], BF16, name="inp_sb")
+            nc.sync.dma_start(
+                out=inp_b[:].rearrange("p (half odd) f -> p half odd f", odd=2),
+                in_=inp[b].rearrange("(half p odd) f -> p half odd f", half=2, odd=2),
+            )
+            inp_sb.append(inp_b)
+        x_sb = []
+        for b in range(IMAGES):
+            x_b = sbuf.tile([P, TILES, SIZE], BF16, name="x_sb")
+            nc.sync.dma_start(out=x_b[:], in_=x[b].rearrange("(p j) d -> p j d", j=TILES))
+            x_sb.append(x_b)
+
+        e_sb = []
+        rowsum = []
+        for b in range(IMAGES):
+            e_b = sbuf.tile([P, TILES, SIZE], BF16, name="e_sb")
+            rowsum_b = sbuf.tile([P, TILES], F32, name="rowsum")
+            for h in range(2):
+                two = slice(2 * h, 2 * h + 2)
+                fold_256 = halves.tile([P, 2, 256], BF16, name="fold_256")
+                fold_128 = halves.tile([P, 2, 128], BF16, name="fold_128")
+                fold_64 = halves.tile([P, 2, 64], BF16, name="fold_64")
+                negmax = halves.tile([P, 2], F32, name="negmax")
+                nc.vector.tensor_tensor(
+                    out=fold_256[:], in0=xwx_sb[b][:, two, 0:256], in1=xwx_sb[b][:, two, 256:512], op=ALU.max
+                )
+                nc.vector.tensor_tensor(
+                    out=fold_128[:], in0=fold_256[:, :, 0:128], in1=fold_256[:, :, 128:256], op=ALU.max
+                )
+                nc.vector.tensor_tensor(
+                    out=fold_64[:], in0=fold_128[:, :, 0:64], in1=fold_128[:, :, 64:128], op=ALU.max
+                )
+                nc.vector.tensor_reduce(
+                    out=negmax[:], in_=fold_64[:], axis=AXIS.X, op=ALU.max, negate=True
+                )
+                for i in range(2):
+                    j = 2 * h + i
+                    nc.scalar.activation(
+                        out=e_b[:, j, :],
+                        in_=xwx_sb[b][:, j, :],
+                        func=ACT.Exp,
+                        bias=negmax[:, i : i + 1],
+                        scale=1.0,
+                        accum_out=rowsum_b[:, j : j + 1],
+                    )
+            e_sb.append(e_b)
+            rowsum.append(rowsum_b)
+
+        def contraction_to_partitions(rows, pool, name):
+            grouped = pool.tile([P, PACK * SIZE], BF16, name=name + "_grouped", align_bytes=64)
+            k_to_partitions(nc, psum_transposed, rows, identity[:], grouped[:])
+            return grouped
+
+        def first_matmul(inp_q, v_q):
+            inp_codes, inp_scales = inp_q
+            v_codes, v_scales = v_q
+            squares = sbuf.tile([P, SIZE, TILES], F32, name="squares")
+            for quarter in range(TILES):
+                features = slice(quarter * P, (quarter + 1) * P)
+                u_bank = psum_u.tile([P, TILES, P], F32, name="u_bank")
+                for m in range(TILES):
+                    patches = slice(m * P, (m + 1) * P)
+                    nc.tensor.matmul_mx(
+                        out=u_bank[:, m, :],
+                        lhsT=inp_codes[:, patches].bitcast(FP8X4),
+                        lhsT_scale=inp_scales[:, patches],
+                        rhs=v_codes[:, features].bitcast(FP8X4),
+                        rhs_scale=v_scales[:, features],
+                        start=True,
+                        stop=True,
+                    )
+                nc.scalar.activation(
+                    out=squares[:, features, :],
+                    in_=u_bank[:].rearrange("p m d -> p d m"),
+                    func=ACT.Square,
+                )
+            return squares
+
+        def root(squares):
+            vx_grouped = sbuf.tile([P, PACK * SIZE], BF16, name="vx_grouped", align_bytes=64)
+            nc.scalar.activation(
+                out=vx_grouped[:],
+                in_=squares[:].rearrange("p d m -> p (d m)"),
+                func=ACT.Sqrt,
+                bias=eps[:],
+                scale=1.0,
+            )
+            return vx_grouped
+
+        def second_matmul(b, e_q, vx_q):
+            e_codes, e_scales = e_q
+            vx_codes, vx_scales = vx_q
+            inverse = sbuf.tile([P, TILES], F32, name="inverse")
+            nc.vector.reciprocal(out=inverse[:], in_=rowsum[b][:])
+            out_sb = sbuf.tile([P, TILES, SIZE], F32, name="out_sb")
+            for j in range(TILES):
+                queries = slice(j * P, (j + 1) * P)
+                t_bank = psum_t.tile([P, SIZE], F32, name="t_bank")
+                nc.tensor.matmul_mx(
+                    out=t_bank[:],
+                    lhsT=e_codes[:, queries].bitcast(FP8X4),
+                    lhsT_scale=e_scales[:, queries],
+                    rhs=vx_codes[:].bitcast(FP8X4),
+                    rhs_scale=vx_scales[:],
+                    start=True,
+                    stop=True,
+                )
+                nc.vector.scalar_tensor_tensor(
+                    out=out_sb[:, j, :],
+                    in0=t_bank[:],
+                    scalar=inverse[:, j : j + 1],
+                    in1=x_sb[b][:, j, :],
+                    op0=ALU.mult,
+                    op1=ALU.add,
+                )
+            nc.sync.dma_start(out=out[b].rearrange("(p j) d -> p j d", j=TILES), in_=out_sb[:])
+
+        v_grouped = contraction_to_partitions(v_sb[:], const, "v")
+        inp_grouped = contraction_to_partitions(inp_sb[0][:], sbuf, "inp")
+        v_q = quantise(nc, const, v_grouped[:], "v")
+        inp_q = quantise(nc, sbuf, inp_grouped[:], "inp")
+        squares = first_matmul(inp_q, v_q)
+        for b in range(IMAGES):
+            e_grouped = contraction_to_partitions(e_sb[b][:], sbuf, "e")
+            if b + 1 < IMAGES:
+                inp_grouped = contraction_to_partitions(inp_sb[b + 1][:], sbuf, "inp")
+            e_q = quantise(nc, sbuf, e_grouped[:], "e")
+            if b + 1 < IMAGES:
+                inp_q = quantise(nc, sbuf, inp_grouped[:], "inp")
+            vx_grouped = root(squares)
+            if b + 1 < IMAGES:
+                squares = first_matmul(inp_q, v_q)
+            vx_q = quantise(nc, sbuf, vx_grouped[:], "vx")
+            second_matmul(b, e_q, vx_q)

@@ -17,37 +17,9 @@ PACK = 4
 IMAGES = 3
 SIZE = 512
 TILES = SIZE // P
-WORDS = SIZE // 2
 EPS = 1e-8
 
 FLOPS = 2 * 2 * IMAGES * SIZE * SIZE * SIZE
-
-
-def k_to_partitions(nc, psum, rows, identity, grouped):
-    row_words = rows.bitcast(F32)
-    grouped_words = grouped.bitcast(F32).rearrange(
-        "w (tile r half) -> w tile r half", tile=TILES, half=2
-    )
-    for pair in range(TILES // 2):
-        bank = psum.tile([P, 2, 2, P], F32, name="transposed")
-        for tile_in_pair in range(2):
-            for half in range(2):
-                nc.tensor.transpose(
-                    bank[:, tile_in_pair, half, :],
-                    row_words[:, 2 * pair + tile_in_pair, half * P : (half + 1) * P],
-                    identity,
-                )
-        nc.vector.tensor_copy(
-            out=grouped_words[:, 2 * pair : 2 * pair + 2, :, :],
-            in_=bank[:].rearrange("w tile half r -> w tile r half"),
-        )
-
-
-def quantise(nc, pool, grouped, name):
-    codes = pool.tile([P, SIZE], U32, name=name + "_codes", align_bytes=64)
-    scales = pool.tile([P, SIZE], U8, name=name + "_scales", align_bytes=64)
-    nc.vector.quantize_mx(out=codes[:].bitcast(FP8X4), scales=scales[:], in_=grouped)
-    return codes, scales
 
 
 def tile_quantumattentionblock_pb_kernel(tc, xwx, inp, V, x, out):
@@ -55,24 +27,29 @@ def tile_quantumattentionblock_pb_kernel(tc, xwx, inp, V, x, out):
     with ExitStack() as ctx:
         const = ctx.enter_context(tc.tile_pool(name="const", bufs=1))
         sbuf = ctx.enter_context(tc.tile_pool(name="sbuf", bufs=IMAGES))
-        halves = ctx.enter_context(tc.tile_pool(name="halves", bufs=2 * IMAGES))
-        psum_transposed = ctx.enter_context(tc.psum_pool(name="psum_transposed", bufs=2))
-        psum_u = ctx.enter_context(tc.psum_pool(name="psum_u", bufs=3))
-        psum_t = ctx.enter_context(tc.psum_pool(name="psum_t", bufs=3))
+        pieces = ctx.enter_context(tc.tile_pool(name="pieces", bufs=IMAGES + 1))
+        psum_vector = ctx.enter_context(tc.psum_pool(name="psum_vector", bufs=4))
+        psum_scalar = ctx.enter_context(tc.psum_pool(name="psum_scalar", bufs=4))
 
         identity = const.tile([P, P], F32, name="identity")
         make_identity(nc, identity[:])
         eps = const.tile([P, 1], F32, name="eps")
         nc.vector.memset(eps[:], EPS)
 
+        def softmax_pieces(b):
+            return 2 if b == 0 else 1
+
+        def end_pieces(b):
+            return 2 if b == IMAGES - 1 else 1
+
         xwx_sb = []
         for b in range(IMAGES):
             xwx_b = sbuf.tile([P, TILES, SIZE], BF16, name="xwx_sb")
             xwx_rows = xwx[b].rearrange("(p j) n -> p j n", j=TILES)
-            for h in range(2):
-                nc.sync.dma_start(
-                    out=xwx_b[:, 2 * h : 2 * h + 2, :], in_=xwx_rows[:, 2 * h : 2 * h + 2, :]
-                )
+            tiles_in_piece = TILES // softmax_pieces(b)
+            for first in range(0, TILES, tiles_in_piece):
+                some = slice(first, first + tiles_in_piece)
+                nc.sync.dma_start(out=xwx_b[:, some, :], in_=xwx_rows[:, some, :])
             xwx_sb.append(xwx_b)
         v_sb = const.tile([P, TILES, SIZE], BF16, name="v_sb")
         nc.sync.dma_start(out=v_sb[:], in_=V.rearrange("(r p) f -> p r f", p=P))
@@ -95,14 +72,18 @@ def tile_quantumattentionblock_pb_kernel(tc, xwx, inp, V, x, out):
         for b in range(IMAGES):
             e_b = sbuf.tile([P, TILES, SIZE], BF16, name="e_sb")
             rowsum_b = sbuf.tile([P, TILES], F32, name="rowsum")
-            for h in range(2):
-                two = slice(2 * h, 2 * h + 2)
-                fold_256 = halves.tile([P, 2, 256], BF16, name="fold_256")
-                fold_128 = halves.tile([P, 2, 128], BF16, name="fold_128")
-                fold_64 = halves.tile([P, 2, 64], BF16, name="fold_64")
-                negmax = halves.tile([P, 2], F32, name="negmax")
+            tiles_in_piece = TILES // softmax_pieces(b)
+            for first in range(0, TILES, tiles_in_piece):
+                some = slice(first, first + tiles_in_piece)
+                fold_256 = pieces.tile([P, tiles_in_piece, 256], BF16, name="fold_256")
+                fold_128 = pieces.tile([P, tiles_in_piece, 128], BF16, name="fold_128")
+                fold_64 = pieces.tile([P, tiles_in_piece, 64], BF16, name="fold_64")
+                negmax = pieces.tile([P, tiles_in_piece], F32, name="negmax")
                 nc.vector.tensor_tensor(
-                    out=fold_256[:], in0=xwx_sb[b][:, two, 0:256], in1=xwx_sb[b][:, two, 256:512], op=ALU.max
+                    out=fold_256[:],
+                    in0=xwx_sb[b][:, some, 0:256],
+                    in1=xwx_sb[b][:, some, 256:512],
+                    op=ALU.max,
                 )
                 nc.vector.tensor_tensor(
                     out=fold_128[:], in0=fold_256[:, :, 0:128], in1=fold_256[:, :, 128:256], op=ALU.max
@@ -113,8 +94,8 @@ def tile_quantumattentionblock_pb_kernel(tc, xwx, inp, V, x, out):
                 nc.vector.tensor_reduce(
                     out=negmax[:], in_=fold_64[:], axis=AXIS.X, op=ALU.max, negate=True
                 )
-                for i in range(2):
-                    j = 2 * h + i
+                for i in range(tiles_in_piece):
+                    j = first + i
                     nc.scalar.activation(
                         out=e_b[:, j, :],
                         in_=xwx_sb[b][:, j, :],
@@ -126,56 +107,87 @@ def tile_quantumattentionblock_pb_kernel(tc, xwx, inp, V, x, out):
             e_sb.append(e_b)
             rowsum.append(rowsum_b)
 
-        def contraction_to_partitions(rows, pool, name):
+        def transposes(rows):
+            row_words = rows.bitcast(F32)
+            banks = []
+            for pair in range(TILES // 2):
+                bank = psum_vector.tile([P, 2, 2, P], F32, name="transposed", tag="for_vector")
+                for tile_in_pair in range(2):
+                    for half in range(2):
+                        nc.tensor.transpose(
+                            bank[:, tile_in_pair, half, :],
+                            row_words[:, 2 * pair + tile_in_pair, half * P : (half + 1) * P],
+                            identity[:],
+                        )
+                banks.append(bank)
+            return banks
+
+        def copy_out(banks, pool, name):
             grouped = pool.tile([P, PACK * SIZE], BF16, name=name + "_grouped", align_bytes=64)
-            k_to_partitions(nc, psum_transposed, rows, identity[:], grouped[:])
+            grouped_words = grouped[:].bitcast(F32).rearrange(
+                "w (tile r half) -> w tile r half", tile=TILES, half=2
+            )
+            for pair in range(TILES // 2):
+                nc.vector.tensor_copy(
+                    out=grouped_words[:, 2 * pair : 2 * pair + 2, :, :],
+                    in_=banks[pair][:].rearrange("w tile half r -> w tile r half"),
+                )
             return grouped
 
-        def first_matmul(inp_q, v_q):
+        def quantise(grouped, columns, pool, name):
+            codes = pool.tile([P, columns], U32, name=name + "_codes", align_bytes=64)
+            scales = pool.tile([P, columns], U8, name=name + "_scales", align_bytes=64)
+            nc.vector.quantize_mx(out=codes[:].bitcast(FP8X4), scales=scales[:], in_=grouped)
+            return codes, scales
+
+        def vx_of(b, inp_q):
             inp_codes, inp_scales = inp_q
             v_codes, v_scales = v_q
             squares = sbuf.tile([P, SIZE, TILES], F32, name="squares")
-            for quarter in range(TILES):
-                features = slice(quarter * P, (quarter + 1) * P)
-                u_bank = psum_u.tile([P, TILES, P], F32, name="u_bank")
-                for m in range(TILES):
-                    patches = slice(m * P, (m + 1) * P)
-                    nc.tensor.matmul_mx(
-                        out=u_bank[:, m, :],
-                        lhsT=inp_codes[:, patches].bitcast(FP8X4),
-                        lhsT_scale=inp_scales[:, patches],
-                        rhs=v_codes[:, features].bitcast(FP8X4),
-                        rhs_scale=v_scales[:, features],
-                        start=True,
-                        stop=True,
+            vx_grouped = sbuf.tile([P, SIZE, PACK], BF16, name="vx_grouped", align_bytes=64)
+            width = SIZE // end_pieces(b)
+            for first in range(0, SIZE, width):
+                for start in range(first, first + width, P):
+                    features = slice(start, start + P)
+                    u_bank = psum_scalar.tile([P, TILES, P], F32, name="u_bank")
+                    for m in range(TILES):
+                        patches = slice(m * P, (m + 1) * P)
+                        nc.tensor.matmul_mx(
+                            out=u_bank[:, m, :],
+                            lhsT=inp_codes[:, patches].bitcast(FP8X4),
+                            lhsT_scale=inp_scales[:, patches],
+                            rhs=v_codes[:, features].bitcast(FP8X4),
+                            rhs_scale=v_scales[:, features],
+                            start=True,
+                            stop=True,
+                        )
+                    nc.scalar.activation(
+                        out=squares[:, features, :],
+                        in_=u_bank[:].rearrange("p m d -> p d m"),
+                        func=ACT.Square,
                     )
                 nc.scalar.activation(
-                    out=squares[:, features, :],
-                    in_=u_bank[:].rearrange("p m d -> p d m"),
-                    func=ACT.Square,
+                    out=vx_grouped[:, first : first + width, :],
+                    in_=squares[:, first : first + width, :],
+                    func=ACT.Sqrt,
+                    bias=eps[:],
+                    scale=1.0,
                 )
-            return squares
-
-        def root(squares):
-            vx_grouped = sbuf.tile([P, PACK * SIZE], BF16, name="vx_grouped", align_bytes=64)
-            nc.scalar.activation(
-                out=vx_grouped[:],
-                in_=squares[:].rearrange("p d m -> p (d m)"),
-                func=ACT.Sqrt,
-                bias=eps[:],
-                scale=1.0,
-            )
             return vx_grouped
 
-        def second_matmul(b, e_q, vx_q):
+        def quantise_vx(b, first):
+            width = SIZE // end_pieces(b)
+            some = vx_grouped[b][:, first : first + width, :]
+            return quantise(some.rearrange("p d m -> p (d m)"), width, pieces, "vx")
+
+        def second_matmul(b, e_q, vx_q, first):
             e_codes, e_scales = e_q
             vx_codes, vx_scales = vx_q
-            inverse = sbuf.tile([P, TILES], F32, name="inverse")
-            nc.vector.reciprocal(out=inverse[:], in_=rowsum[b][:])
-            out_sb = sbuf.tile([P, TILES, SIZE], F32, name="out_sb")
+            width = SIZE // end_pieces(b)
+            out_rows = out[b].rearrange("(p j) d -> p j d", j=TILES)
             for j in range(TILES):
                 queries = slice(j * P, (j + 1) * P)
-                t_bank = psum_t.tile([P, SIZE], F32, name="t_bank")
+                t_bank = psum_vector.tile([P, width], F32, name="t_bank", tag="for_vector")
                 nc.tensor.matmul_mx(
                     out=t_bank[:],
                     lhsT=e_codes[:, queries].bitcast(FP8X4),
@@ -185,30 +197,50 @@ def tile_quantumattentionblock_pb_kernel(tc, xwx, inp, V, x, out):
                     start=True,
                     stop=True,
                 )
+                out_sb = pieces.tile([P, width], F32, name="out_sb", bufs=2 * TILES)
                 nc.vector.scalar_tensor_tensor(
-                    out=out_sb[:, j, :],
+                    out=out_sb[:],
                     in0=t_bank[:],
-                    scalar=inverse[:, j : j + 1],
-                    in1=x_sb[b][:, j, :],
+                    scalar=inverse[b][:, j : j + 1],
+                    in1=x_sb[b][:, j, first : first + width],
                     op0=ALU.mult,
                     op1=ALU.add,
                 )
-            nc.sync.dma_start(out=out[b].rearrange("(p j) d -> p j d", j=TILES), in_=out_sb[:])
+                nc.sync.dma_start(out=out_rows[:, j, first : first + width], in_=out_sb[:])
 
-        v_grouped = contraction_to_partitions(v_sb[:], const, "v")
-        inp_grouped = contraction_to_partitions(inp_sb[0][:], sbuf, "inp")
-        v_q = quantise(nc, const, v_grouped[:], "v")
-        inp_q = quantise(nc, sbuf, inp_grouped[:], "inp")
-        squares = first_matmul(inp_q, v_q)
+        v_grouped = copy_out(transposes(v_sb[:]), const, "v")
+        inp_grouped = copy_out(transposes(inp_sb[0][:]), sbuf, "inp")
+        v_q = quantise(v_grouped[:], SIZE, const, "v")
+        inp_q = quantise(inp_grouped[:], SIZE, sbuf, "inp")
+        vx_grouped = [vx_of(0, inp_q)]
+        e_grouped = copy_out(transposes(e_sb[0][:]), sbuf, "e")
+        inp_banks = transposes(inp_sb[1][:])
+        inverse = []
         for b in range(IMAGES):
-            e_grouped = contraction_to_partitions(e_sb[b][:], sbuf, "e")
-            if b + 1 < IMAGES:
-                inp_grouped = contraction_to_partitions(inp_sb[b + 1][:], sbuf, "inp")
-            e_q = quantise(nc, sbuf, e_grouped[:], "e")
-            if b + 1 < IMAGES:
-                inp_q = quantise(nc, sbuf, inp_grouped[:], "inp")
-            vx_grouped = root(squares)
-            if b + 1 < IMAGES:
-                squares = first_matmul(inp_q, v_q)
-            vx_q = quantise(nc, sbuf, vx_grouped[:], "vx")
-            second_matmul(b, e_q, vx_q)
+            inverse_b = sbuf.tile([P, TILES], F32, name="inverse")
+            nc.vector.reciprocal(out=inverse_b[:], in_=rowsum[b][:])
+            inverse.append(inverse_b)
+
+        e_q = [None] * IMAGES
+        for b in range(IMAGES):
+            following = b + 1
+            if following < IMAGES:
+                inp_grouped = copy_out(inp_banks, sbuf, "inp")
+                e_banks = transposes(e_sb[following][:])
+            e_q[b] = quantise(e_grouped[:], SIZE, sbuf, "e")
+            if b > 0:
+                vx_q = quantise_vx(b - 1, 0)
+            if following < IMAGES:
+                e_grouped = copy_out(e_banks, sbuf, "e")
+                if following + 1 < IMAGES:
+                    inp_banks = transposes(inp_sb[following + 1][:])
+                inp_q = quantise(inp_grouped[:], SIZE, sbuf, "inp")
+            if b > 0:
+                second_matmul(b - 1, e_q[b - 1], vx_q, 0)
+            if following < IMAGES:
+                vx_grouped.append(vx_of(following, inp_q))
+
+        last = IMAGES - 1
+        for first in range(0, SIZE, SIZE // end_pieces(last)):
+            vx_q = quantise_vx(last, first)
+            second_matmul(last, e_q[last], vx_q, first)

@@ -140,35 +140,35 @@ def tile_quantumattentionblock_pb_kernel(tc, xwx, inp, V, x, out):
             nc.vector.quantize_mx(out=codes[:].bitcast(FP8X4), scales=scales[:], in_=grouped)
             return codes, scales
 
-        def vx_of(b, inp_q):
+        def vx_of(inp_q):
             inp_codes, inp_scales = inp_q
             v_codes, v_scales = v_q
             squares = sbuf.tile([P, SIZE, TILES], F32, name="squares")
             vx_grouped = sbuf.tile([P, SIZE, PACK], BF16, name="vx_grouped", align_bytes=64)
-            width = SIZE // end_pieces(b)
-            for first in range(0, SIZE, width):
-                for start in range(first, first + width, P):
-                    features = slice(start, start + P)
-                    u_bank = psum_scalar.tile([P, TILES, P], F32, name="u_bank")
-                    for m in range(TILES):
-                        patches = slice(m * P, (m + 1) * P)
-                        nc.tensor.matmul_mx(
-                            out=u_bank[:, m, :],
-                            lhsT=inp_codes[:, patches].bitcast(FP8X4),
-                            lhsT_scale=inp_scales[:, patches],
-                            rhs=v_codes[:, features].bitcast(FP8X4),
-                            rhs_scale=v_scales[:, features],
-                            start=True,
-                            stop=True,
-                        )
-                    nc.scalar.activation(
-                        out=squares[:, features, :],
-                        in_=u_bank[:].rearrange("p m d -> p d m"),
-                        func=ACT.Square,
+            for start in range(0, SIZE, P):
+                features = slice(start, start + P)
+                u_bank = psum_scalar.tile([P, TILES, P], F32, name="u_bank")
+                for m in range(TILES):
+                    patches = slice(m * P, (m + 1) * P)
+                    nc.tensor.matmul_mx(
+                        out=u_bank[:, m, :],
+                        lhsT=inp_codes[:, patches].bitcast(FP8X4),
+                        lhsT_scale=inp_scales[:, patches],
+                        rhs=v_codes[:, features].bitcast(FP8X4),
+                        rhs_scale=v_scales[:, features],
+                        start=True,
+                        stop=True,
                     )
                 nc.scalar.activation(
-                    out=vx_grouped[:, first : first + width, :],
-                    in_=squares[:, first : first + width, :],
+                    out=squares[:, features, :],
+                    in_=u_bank[:].rearrange("p m d -> p d m"),
+                    func=ACT.Square,
+                )
+            for start in range(0, SIZE, SIZE // 2):
+                features = slice(start, start + SIZE // 2)
+                nc.scalar.activation(
+                    out=vx_grouped[:, features, :],
+                    in_=squares[:, features, :],
                     func=ACT.Sqrt,
                     bias=eps[:],
                     scale=1.0,
@@ -212,7 +212,7 @@ def tile_quantumattentionblock_pb_kernel(tc, xwx, inp, V, x, out):
         inp_grouped = copy_out(transposes(inp_sb[0][:]), sbuf, "inp")
         v_q = quantise(v_grouped[:], SIZE, const, "v")
         inp_q = quantise(inp_grouped[:], SIZE, sbuf, "inp")
-        vx_grouped = [vx_of(0, inp_q)]
+        vx_grouped = [vx_of(inp_q)]
         e_grouped = copy_out(transposes(e_sb[0][:]), sbuf, "e")
         inp_banks = transposes(inp_sb[1][:])
         inverse = []
@@ -238,7 +238,7 @@ def tile_quantumattentionblock_pb_kernel(tc, xwx, inp, V, x, out):
             if b > 0:
                 second_matmul(b - 1, e_q[b - 1], vx_q, 0)
             if following < IMAGES:
-                vx_grouped.append(vx_of(following, inp_q))
+                vx_grouped.append(vx_of(inp_q))
 
         last = IMAGES - 1
         for first in range(0, SIZE, SIZE // end_pieces(last)):

@@ -106,6 +106,8 @@ def tile_quantumattentionblock_pb_kernel(tc, xwx, inp, V, x, out):
                     )
             e_sb.append(e_b)
             rowsum.append(rowsum_b)
+        warm = const.tile([P, 1], F32, name="warm")
+        nc.scalar.activation(out=warm[:], in_=rowsum[IMAGES - 1][:, TILES - 1 : TILES], func=ACT.Sqrt)
 
         def transposes(rows):
             row_words = rows.bitcast(F32)
@@ -140,35 +142,35 @@ def tile_quantumattentionblock_pb_kernel(tc, xwx, inp, V, x, out):
             nc.vector.quantize_mx(out=codes[:].bitcast(FP8X4), scales=scales[:], in_=grouped)
             return codes, scales
 
-        def vx_of(inp_q):
+        def vx_of(b, inp_q):
             inp_codes, inp_scales = inp_q
             v_codes, v_scales = v_q
             squares = sbuf.tile([P, SIZE, TILES], F32, name="squares")
             vx_grouped = sbuf.tile([P, SIZE, PACK], BF16, name="vx_grouped", align_bytes=64)
-            for start in range(0, SIZE, P):
-                features = slice(start, start + P)
-                u_bank = psum_scalar.tile([P, TILES, P], F32, name="u_bank")
-                for m in range(TILES):
-                    patches = slice(m * P, (m + 1) * P)
-                    nc.tensor.matmul_mx(
-                        out=u_bank[:, m, :],
-                        lhsT=inp_codes[:, patches].bitcast(FP8X4),
-                        lhsT_scale=inp_scales[:, patches],
-                        rhs=v_codes[:, features].bitcast(FP8X4),
-                        rhs_scale=v_scales[:, features],
-                        start=True,
-                        stop=True,
+            width = SIZE // end_pieces(b)
+            for first in range(0, SIZE, width):
+                for start in range(first, first + width, P):
+                    features = slice(start, start + P)
+                    u_bank = psum_scalar.tile([P, TILES, P], F32, name="u_bank")
+                    for m in range(TILES):
+                        patches = slice(m * P, (m + 1) * P)
+                        nc.tensor.matmul_mx(
+                            out=u_bank[:, m, :],
+                            lhsT=inp_codes[:, patches].bitcast(FP8X4),
+                            lhsT_scale=inp_scales[:, patches],
+                            rhs=v_codes[:, features].bitcast(FP8X4),
+                            rhs_scale=v_scales[:, features],
+                            start=True,
+                            stop=True,
+                        )
+                    nc.scalar.activation(
+                        out=squares[:, features, :],
+                        in_=u_bank[:].rearrange("p m d -> p d m"),
+                        func=ACT.Square,
                     )
                 nc.scalar.activation(
-                    out=squares[:, features, :],
-                    in_=u_bank[:].rearrange("p m d -> p d m"),
-                    func=ACT.Square,
-                )
-            for start in range(0, SIZE, SIZE // 2):
-                features = slice(start, start + SIZE // 2)
-                nc.scalar.activation(
-                    out=vx_grouped[:, features, :],
-                    in_=squares[:, features, :],
+                    out=vx_grouped[:, first : first + width, :],
+                    in_=squares[:, first : first + width, :],
                     func=ACT.Sqrt,
                     bias=eps[:],
                     scale=1.0,
@@ -180,12 +182,12 @@ def tile_quantumattentionblock_pb_kernel(tc, xwx, inp, V, x, out):
             some = vx_grouped[b][:, first : first + width, :]
             return quantise(some.rearrange("p d m -> p (d m)"), width, pieces, "vx")
 
-        def second_matmul(b, e_q, vx_q, first):
+        def second_matmul(b, e_q, vx_q, first, row_tiles):
             e_codes, e_scales = e_q
             vx_codes, vx_scales = vx_q
             width = SIZE // end_pieces(b)
             out_rows = out[b].rearrange("(p j) d -> p j d", j=TILES)
-            for j in range(TILES):
+            for j in row_tiles:
                 queries = slice(j * P, (j + 1) * P)
                 t_bank = psum_vector.tile([P, width], F32, name="t_bank", tag="for_vector")
                 nc.tensor.matmul_mx(
@@ -212,7 +214,7 @@ def tile_quantumattentionblock_pb_kernel(tc, xwx, inp, V, x, out):
         inp_grouped = copy_out(transposes(inp_sb[0][:]), sbuf, "inp")
         v_q = quantise(v_grouped[:], SIZE, const, "v")
         inp_q = quantise(inp_grouped[:], SIZE, sbuf, "inp")
-        vx_grouped = [vx_of(inp_q)]
+        vx_grouped = [vx_of(0, inp_q)]
         e_grouped = copy_out(transposes(e_sb[0][:]), sbuf, "e")
         inp_banks = transposes(inp_sb[1][:])
         inverse = []
@@ -221,26 +223,32 @@ def tile_quantumattentionblock_pb_kernel(tc, xwx, inp, V, x, out):
             nc.vector.reciprocal(out=inverse_b[:], in_=rowsum[b][:])
             inverse.append(inverse_b)
 
-        e_q = [None] * IMAGES
-        for b in range(IMAGES):
-            following = b + 1
-            if following < IMAGES:
-                inp_grouped = copy_out(inp_banks, sbuf, "inp")
-                e_banks = transposes(e_sb[following][:])
-            e_q[b] = quantise(e_grouped[:], SIZE, sbuf, "e")
+        e_q = []
+        for b in range(IMAGES - 1):
+            inp_grouped = copy_out(inp_banks, sbuf, "inp")
+            e_banks = transposes(e_sb[b + 1][:])
+            e_q.append(quantise(e_grouped[:], SIZE, sbuf, "e"))
             if b > 0:
                 vx_q = quantise_vx(b - 1, 0)
-            if following < IMAGES:
-                e_grouped = copy_out(e_banks, sbuf, "e")
-                if following + 1 < IMAGES:
-                    inp_banks = transposes(inp_sb[following + 1][:])
-                inp_q = quantise(inp_grouped[:], SIZE, sbuf, "inp")
+            e_grouped = copy_out(e_banks, sbuf, "e")
+            if b + 2 < IMAGES:
+                inp_banks = transposes(inp_sb[b + 2][:])
+            inp_q = quantise(inp_grouped[:], SIZE, sbuf, "inp")
             if b > 0:
-                second_matmul(b - 1, e_q[b - 1], vx_q, 0)
-            if following < IMAGES:
-                vx_grouped.append(vx_of(inp_q))
+                second_matmul(b - 1, e_q[b - 1], vx_q, 0, range(TILES))
+            vx_grouped.append(vx_of(b + 1, inp_q))
 
-        last = IMAGES - 1
-        for first in range(0, SIZE, SIZE // end_pieces(last)):
-            vx_q = quantise_vx(last, first)
-            second_matmul(last, e_q[last], vx_q, first)
+        ends = [
+            (b, first)
+            for b in range(IMAGES - 2, IMAGES)
+            for first in range(0, SIZE, SIZE // end_pieces(b))
+        ]
+        vx_q = quantise_vx(ends[0][0], ends[0][1])
+        e_q.append(quantise(e_grouped[:], SIZE, sbuf, "e"))
+        for k in range(len(ends)):
+            b, first = ends[k]
+            second_matmul(b, e_q[b], vx_q, first, range(0, TILES // 2))
+            if k + 1 < len(ends):
+                following_q = quantise_vx(ends[k + 1][0], ends[k + 1][1])
+            second_matmul(b, e_q[b], vx_q, first, range(TILES // 2, TILES))
+            vx_q = following_q

@@ -17,6 +17,7 @@ PACK = 4
 IMAGES = 3
 SIZE = 512
 TILES = SIZE // P
+PAIRS = TILES // 2
 EPS = 1e-8
 
 FLOPS = 2 * 2 * IMAGES * SIZE * SIZE * SIZE
@@ -36,105 +37,85 @@ def tile_quantumattentionblock_pb_kernel(tc, xwx, inp, V, x, out):
         eps = const.tile([P, 1], F32, name="eps")
         nc.vector.memset(eps[:], EPS)
 
-        def softmax_pieces(b):
-            return 2 if b == 0 else 1
+        ctx.enter_context(tc.manual_schedule())
 
-        def end_pieces(b):
-            return 2 if b == IMAGES - 1 else 1
-
-        xwx_sb = []
-        for b in range(IMAGES):
-            xwx_b = sbuf.tile([P, TILES, SIZE], BF16, name="xwx_sb")
-            xwx_rows = xwx[b].rearrange("(p j) n -> p j n", j=TILES)
-            tiles_in_piece = TILES // softmax_pieces(b)
-            for first in range(0, TILES, tiles_in_piece):
-                some = slice(first, first + tiles_in_piece)
-                nc.sync.dma_start(out=xwx_b[:, some, :], in_=xwx_rows[:, some, :])
-            xwx_sb.append(xwx_b)
+        xwx_sb = [sbuf.tile([P, TILES, SIZE], BF16, name="xwx_sb") for b in range(IMAGES)]
+        inp_sb = [sbuf.tile([P, TILES, SIZE], BF16, name="inp_sb") for b in range(IMAGES)]
+        x_sb = [sbuf.tile([P, TILES, SIZE], BF16, name="x_sb") for b in range(IMAGES)]
         v_sb = const.tile([P, TILES, SIZE], BF16, name="v_sb")
-        nc.sync.dma_start(out=v_sb[:], in_=V.rearrange("(r p) f -> p r f", p=P))
-        inp_sb = []
-        for b in range(IMAGES):
-            inp_b = sbuf.tile([P, TILES, SIZE], BF16, name="inp_sb")
+
+        def load_xwx(b, tiles):
+            rows = xwx[b].rearrange("(p j) n -> p j n", j=TILES)
+            nc.sync.dma_start(out=xwx_sb[b][:, tiles, :], in_=rows[:, tiles, :])
+
+        def load_inp(b):
             nc.sync.dma_start(
-                out=inp_b[:].rearrange("p (half odd) f -> p half odd f", odd=2),
+                out=inp_sb[b][:].rearrange("p (half odd) f -> p half odd f", odd=2),
                 in_=inp[b].rearrange("(half p odd) f -> p half odd f", half=2, odd=2),
             )
-            inp_sb.append(inp_b)
-        x_sb = []
-        for b in range(IMAGES):
-            x_b = sbuf.tile([P, TILES, SIZE], BF16, name="x_sb")
-            nc.sync.dma_start(out=x_b[:], in_=x[b].rearrange("(p j) d -> p j d", j=TILES))
-            x_sb.append(x_b)
 
-        e_sb = []
-        rowsum = []
+        load_xwx(0, slice(0, 1))
+        load_xwx(0, slice(1, 2))
+        load_xwx(0, slice(2, 4))
+        load_xwx(1, slice(0, 4))
+        nc.sync.dma_start(out=v_sb[:], in_=V.rearrange("(r p) f -> p r f", p=P))
+        load_inp(0)
+        load_xwx(2, slice(0, 4))
+        load_inp(1)
+        load_inp(2)
         for b in range(IMAGES):
-            e_b = sbuf.tile([P, TILES, SIZE], BF16, name="e_sb")
-            rowsum_b = sbuf.tile([P, TILES], F32, name="rowsum")
-            tiles_in_piece = TILES // softmax_pieces(b)
-            for first in range(0, TILES, tiles_in_piece):
-                some = slice(first, first + tiles_in_piece)
-                fold_256 = pieces.tile([P, tiles_in_piece, 256], BF16, name="fold_256")
-                fold_128 = pieces.tile([P, tiles_in_piece, 128], BF16, name="fold_128")
-                fold_64 = pieces.tile([P, tiles_in_piece, 64], BF16, name="fold_64")
-                negmax = pieces.tile([P, tiles_in_piece], F32, name="negmax")
-                nc.vector.tensor_tensor(
-                    out=fold_256[:],
-                    in0=xwx_sb[b][:, some, 0:256],
-                    in1=xwx_sb[b][:, some, 256:512],
-                    op=ALU.max,
-                )
-                nc.vector.tensor_tensor(
-                    out=fold_128[:], in0=fold_256[:, :, 0:128], in1=fold_256[:, :, 128:256], op=ALU.max
-                )
-                nc.vector.tensor_tensor(
-                    out=fold_64[:], in0=fold_128[:, :, 0:64], in1=fold_128[:, :, 64:128], op=ALU.max
-                )
-                nc.vector.tensor_reduce(
-                    out=negmax[:], in_=fold_64[:], axis=AXIS.X, op=ALU.max, negate=True
-                )
-                for i in range(tiles_in_piece):
-                    j = first + i
-                    nc.scalar.activation(
-                        out=e_b[:, j, :],
-                        in_=xwx_sb[b][:, j, :],
-                        func=ACT.Exp,
-                        bias=negmax[:, i : i + 1],
-                        scale=1.0,
-                        accum_out=rowsum_b[:, j : j + 1],
-                    )
-            e_sb.append(e_b)
-            rowsum.append(rowsum_b)
-        warm = const.tile([P, 1], F32, name="warm")
-        nc.scalar.activation(out=warm[:], in_=rowsum[IMAGES - 1][:, TILES - 1 : TILES], func=ACT.Sqrt)
+            nc.sync.dma_start(out=x_sb[b][:], in_=x[b].rearrange("(p j) d -> p j d", j=TILES))
 
-        def transposes(rows):
+        e_sb = [sbuf.tile([P, TILES, SIZE], BF16, name="e_sb") for b in range(IMAGES)]
+        negmax = [sbuf.tile([P, TILES], F32, name="negmax") for b in range(IMAGES)]
+        rowsum = [sbuf.tile([P, TILES], F32, name="rowsum") for b in range(IMAGES)]
+        inverse = [sbuf.tile([P, TILES], F32, name="inverse") for b in range(IMAGES)]
+        squares = [sbuf.tile([P, SIZE, TILES], F32, name="squares") for b in range(IMAGES)]
+        vx_grouped = [
+            sbuf.tile([P, SIZE, PACK], BF16, name="vx_grouped", align_bytes=64) for b in range(IMAGES)
+        ]
+
+        def fold(rows, name):
+            width = rows.shape[2] // 2
+            folded = pieces.tile([P, rows.shape[1], width], BF16, name=name)
+            nc.vector.tensor_tensor(
+                out=folded[:], in0=rows[:, :, 0:width], in1=rows[:, :, width : 2 * width], op=ALU.max
+            )
+            return folded
+
+        def reduce_max(rows, b, tiles):
+            nc.vector.tensor_reduce(out=negmax[b][:, tiles], in_=rows, axis=AXIS.X, op=ALU.max, negate=True)
+
+        def exp(b, j):
+            nc.scalar.activation(
+                out=e_sb[b][:, j, :],
+                in_=xwx_sb[b][:, j, :],
+                func=ACT.Exp,
+                bias=negmax[b][:, j : j + 1],
+                scale=1.0,
+                accum_out=rowsum[b][:, j : j + 1],
+            )
+
+        def transpose(rows, pair):
             row_words = rows.bitcast(F32)
-            banks = []
-            for pair in range(TILES // 2):
-                bank = psum_vector.tile([P, 2, 2, P], F32, name="transposed", tag="for_vector")
-                for tile_in_pair in range(2):
-                    for half in range(2):
-                        nc.tensor.transpose(
-                            bank[:, tile_in_pair, half, :],
-                            row_words[:, 2 * pair + tile_in_pair, half * P : (half + 1) * P],
-                            identity[:],
-                        )
-                banks.append(bank)
-            return banks
+            bank = psum_vector.tile([P, 2, 2, P], F32, name="transposed", tag="for_vector")
+            for tile_in_pair in range(2):
+                for half in range(2):
+                    nc.tensor.transpose(
+                        bank[:, tile_in_pair, half, :],
+                        row_words[:, 2 * pair + tile_in_pair, half * P : (half + 1) * P],
+                        identity[:],
+                    )
+            return bank
 
-        def copy_out(banks, pool, name):
-            grouped = pool.tile([P, PACK * SIZE], BF16, name=name + "_grouped", align_bytes=64)
-            grouped_words = grouped[:].bitcast(F32).rearrange(
+        def copy_out(bank, grouped, pair, copy):
+            words = grouped[:].bitcast(F32).rearrange(
                 "w (tile r half) -> w tile r half", tile=TILES, half=2
             )
-            for pair in range(TILES // 2):
-                nc.vector.tensor_copy(
-                    out=grouped_words[:, 2 * pair : 2 * pair + 2, :, :],
-                    in_=banks[pair][:].rearrange("w tile half r -> w tile r half"),
-                )
-            return grouped
+            copy(
+                out=words[:, 2 * pair : 2 * pair + 2, :, :],
+                in_=bank[:].rearrange("w tile half r -> w tile r half"),
+            )
 
         def quantise(grouped, columns, pool, name):
             codes = pool.tile([P, columns], U32, name=name + "_codes", align_bytes=64)
@@ -142,113 +123,166 @@ def tile_quantumattentionblock_pb_kernel(tc, xwx, inp, V, x, out):
             nc.vector.quantize_mx(out=codes[:].bitcast(FP8X4), scales=scales[:], in_=grouped)
             return codes, scales
 
-        def vx_of(b, inp_q):
+        def first_matmul(inp_q, quarter):
             inp_codes, inp_scales = inp_q
             v_codes, v_scales = v_q
-            squares = sbuf.tile([P, SIZE, TILES], F32, name="squares")
-            vx_grouped = sbuf.tile([P, SIZE, PACK], BF16, name="vx_grouped", align_bytes=64)
-            width = SIZE // end_pieces(b)
-            for first in range(0, SIZE, width):
-                for start in range(first, first + width, P):
-                    features = slice(start, start + P)
-                    u_bank = psum_scalar.tile([P, TILES, P], F32, name="u_bank")
-                    for m in range(TILES):
-                        patches = slice(m * P, (m + 1) * P)
-                        nc.tensor.matmul_mx(
-                            out=u_bank[:, m, :],
-                            lhsT=inp_codes[:, patches].bitcast(FP8X4),
-                            lhsT_scale=inp_scales[:, patches],
-                            rhs=v_codes[:, features].bitcast(FP8X4),
-                            rhs_scale=v_scales[:, features],
-                            start=True,
-                            stop=True,
-                        )
-                    nc.scalar.activation(
-                        out=squares[:, features, :],
-                        in_=u_bank[:].rearrange("p m d -> p d m"),
-                        func=ACT.Square,
-                    )
-                nc.scalar.activation(
-                    out=vx_grouped[:, first : first + width, :],
-                    in_=squares[:, first : first + width, :],
-                    func=ACT.Sqrt,
-                    bias=eps[:],
-                    scale=1.0,
-                )
-            return vx_grouped
-
-        def quantise_vx(b, first):
-            width = SIZE // end_pieces(b)
-            some = vx_grouped[b][:, first : first + width, :]
-            return quantise(some.rearrange("p d m -> p (d m)"), width, pieces, "vx")
-
-        def second_matmul(b, e_q, vx_q, first, row_tiles):
-            e_codes, e_scales = e_q
-            vx_codes, vx_scales = vx_q
-            width = SIZE // end_pieces(b)
-            out_rows = out[b].rearrange("(p j) d -> p j d", j=TILES)
-            for j in row_tiles:
-                queries = slice(j * P, (j + 1) * P)
-                t_bank = psum_vector.tile([P, width], F32, name="t_bank", tag="for_vector")
+            features = slice(quarter * P, (quarter + 1) * P)
+            u_bank = psum_scalar.tile([P, TILES, P], F32, name="u_bank")
+            for m in range(TILES):
+                patches = slice(m * P, (m + 1) * P)
                 nc.tensor.matmul_mx(
-                    out=t_bank[:],
-                    lhsT=e_codes[:, queries].bitcast(FP8X4),
-                    lhsT_scale=e_scales[:, queries],
-                    rhs=vx_codes[:].bitcast(FP8X4),
-                    rhs_scale=vx_scales[:],
+                    out=u_bank[:, m, :],
+                    lhsT=inp_codes[:, patches].bitcast(FP8X4),
+                    lhsT_scale=inp_scales[:, patches],
+                    rhs=v_codes[:, features].bitcast(FP8X4),
+                    rhs_scale=v_scales[:, features],
                     start=True,
                     stop=True,
                 )
-                out_sb = pieces.tile([P, width], F32, name="out_sb", bufs=2 * TILES)
-                nc.vector.scalar_tensor_tensor(
-                    out=out_sb[:],
-                    in0=t_bank[:],
-                    scalar=inverse[b][:, j : j + 1],
-                    in1=x_sb[b][:, j, first : first + width],
-                    op0=ALU.mult,
-                    op1=ALU.add,
-                )
-                nc.sync.dma_start(out=out_rows[:, j, first : first + width], in_=out_sb[:])
+            return u_bank
 
-        v_grouped = copy_out(transposes(v_sb[:]), const, "v")
-        inp_grouped = copy_out(transposes(inp_sb[0][:]), sbuf, "inp")
-        v_q = quantise(v_grouped[:], SIZE, const, "v")
-        inp_q = quantise(inp_grouped[:], SIZE, sbuf, "inp")
-        vx_grouped = [vx_of(0, inp_q)]
-        e_grouped = copy_out(transposes(e_sb[0][:]), sbuf, "e")
-        inp_banks = transposes(inp_sb[1][:])
-        inverse = []
-        for b in range(IMAGES):
-            inverse_b = sbuf.tile([P, TILES], F32, name="inverse")
-            nc.vector.reciprocal(out=inverse_b[:], in_=rowsum[b][:])
-            inverse.append(inverse_b)
+        def square(b, quarter, u_bank):
+            nc.scalar.activation(
+                out=squares[b][:, quarter * P : (quarter + 1) * P, :],
+                in_=u_bank[:].rearrange("p m d -> p d m"),
+                func=ACT.Square,
+            )
+
+        def root(b, first, width):
+            nc.scalar.activation(
+                out=vx_grouped[b][:, first : first + width, :],
+                in_=squares[b][:, first : first + width, :],
+                func=ACT.Sqrt,
+                bias=eps[:],
+                scale=1.0,
+            )
+
+        def quantise_vx(b, first, width):
+            some = vx_grouped[b][:, first : first + width, :]
+            return quantise(some.rearrange("p d m -> p (d m)"), width, pieces, "vx")
+
+        def second_matmul(b, j, vx_q, width):
+            e_codes, e_scales = e_q[b]
+            vx_codes, vx_scales = vx_q
+            queries = slice(j * P, (j + 1) * P)
+            t_bank = psum_vector.tile([P, width], F32, name="t_bank", tag="for_vector")
+            nc.tensor.matmul_mx(
+                out=t_bank[:],
+                lhsT=e_codes[:, queries].bitcast(FP8X4),
+                lhsT_scale=e_scales[:, queries],
+                rhs=vx_codes[:].bitcast(FP8X4),
+                rhs_scale=vx_scales[:],
+                start=True,
+                stop=True,
+            )
+            return t_bank
+
+        def finish(b, j, first, width, t_bank):
+            out_sb = pieces.tile([P, width], F32, name="out_sb", bufs=2 * TILES)
+            nc.vector.scalar_tensor_tensor(
+                out=out_sb[:],
+                in0=t_bank[:],
+                scalar=inverse[b][:, j : j + 1],
+                in1=x_sb[b][:, j, first : first + width],
+                op0=ALU.mult,
+                op1=ALU.add,
+            )
+            out_rows = out[b].rearrange("(p j) d -> p j d", j=TILES)
+            nc.sync.dma_start(out=out_rows[:, j, first : first + width], in_=out_sb[:])
+
+        def grouped_tile(pool, name):
+            return pool.tile([P, PACK * SIZE], BF16, name=name + "_grouped", align_bytes=64)
+
+        on_vector = nc.vector.tensor_copy
+        on_scalar = nc.scalar.copy
+
+        warm = const.tile([P, 1], F32, name="warm")
+        nc.scalar.activation(out=warm[:], in_=eps[:], func=ACT.Exp)
+
+        for j in range(TILES):
+            reduce_max(xwx_sb[0][:, j, :], 0, slice(j, j + 1))
+            exp(0, j)
+
+        v_grouped = grouped_tile(const, "v")
+        v_banks = [transpose(v_sb[:], pair) for pair in range(PAIRS)]
+        for pair in range(PAIRS):
+            copy_out(v_banks[pair], v_grouped, pair, on_scalar)
+        half_1 = fold(xwx_sb[1][:], "fold_256")
+        quarter_1 = fold(half_1[:], "fold_128")
+        reduce_max(quarter_1[:], 1, slice(0, TILES))
+        for j in range(TILES):
+            exp(1, j)
+
+        inp_grouped = [grouped_tile(sbuf, "inp") for b in range(IMAGES)]
+        e_grouped = [grouped_tile(sbuf, "e") for b in range(IMAGES)]
+        inp_banks = [transpose(inp_sb[0][:], pair) for pair in range(PAIRS)]
+        half_2 = fold(xwx_sb[2][:], "fold_256")
+        copy_out(inp_banks[0], inp_grouped[0], 0, on_vector)
+        quarter_2 = fold(half_2[:], "fold_128")
+        copy_out(inp_banks[1], inp_grouped[0], 1, on_vector)
+        reduce_max(quarter_2[:], 2, slice(0, TILES))
+        for j in range(TILES):
+            exp(2, j)
+        nc.scalar.activation(out=warm[:], in_=eps[:], func=ACT.Sqrt)
 
         e_q = []
-        for b in range(IMAGES - 1):
-            inp_grouped = copy_out(inp_banks, sbuf, "inp")
-            e_banks = transposes(e_sb[b + 1][:])
-            e_q.append(quantise(e_grouped[:], SIZE, sbuf, "e"))
-            if b > 0:
-                vx_q = quantise_vx(b - 1, 0)
-            e_grouped = copy_out(e_banks, sbuf, "e")
-            if b + 2 < IMAGES:
-                inp_banks = transposes(inp_sb[b + 2][:])
-            inp_q = quantise(inp_grouped[:], SIZE, sbuf, "inp")
-            if b > 0:
-                second_matmul(b - 1, e_q[b - 1], vx_q, 0, range(TILES))
-            vx_grouped.append(vx_of(b + 1, inp_q))
+        v_q = quantise(v_grouped[:], SIZE, const, "v")
+        inp_q = [quantise(inp_grouped[0][:], SIZE, sbuf, "inp")]
+        e_banks = [transpose(e_sb[0][:], pair) for pair in range(PAIRS)]
+        inp_banks = [transpose(inp_sb[1][:], pair) for pair in range(PAIRS)]
 
-        ends = [
-            (b, first)
-            for b in range(IMAGES - 2, IMAGES)
-            for first in range(0, SIZE, SIZE // end_pieces(b))
-        ]
-        vx_q = quantise_vx(ends[0][0], ends[0][1])
-        e_q.append(quantise(e_grouped[:], SIZE, sbuf, "e"))
-        for k in range(len(ends)):
-            b, first = ends[k]
-            second_matmul(b, e_q[b], vx_q, first, range(0, TILES // 2))
-            if k + 1 < len(ends):
-                following_q = quantise_vx(ends[k + 1][0], ends[k + 1][1])
-            second_matmul(b, e_q[b], vx_q, first, range(TILES // 2, TILES))
-            vx_q = following_q
+        for quarter in range(TILES):
+            square(0, quarter, first_matmul(inp_q[0], quarter))
+        root(0, 0, SIZE)
+        for pair in range(PAIRS):
+            copy_out(e_banks[pair], e_grouped[0], pair, on_vector)
+        for pair in range(PAIRS):
+            copy_out(inp_banks[pair], inp_grouped[1], pair, on_vector)
+        e_banks = [transpose(e_sb[1][:], pair) for pair in range(PAIRS)]
+        e_q.append(quantise(e_grouped[0][:], SIZE, sbuf, "e"))
+        inp_q.append(quantise(inp_grouped[1][:], SIZE, sbuf, "inp"))
+        inp_banks = [transpose(inp_sb[2][:], pair) for pair in range(PAIRS)]
+        for b in range(IMAGES):
+            nc.vector.reciprocal(out=inverse[b][:], in_=rowsum[b][:])
+
+        for quarter in range(TILES):
+            square(1, quarter, first_matmul(inp_q[1], quarter))
+        root(1, 0, SIZE)
+        for pair in range(PAIRS):
+            copy_out(e_banks[pair], e_grouped[1], pair, on_vector)
+        for pair in range(PAIRS):
+            copy_out(inp_banks[pair], inp_grouped[2], pair, on_vector)
+        e_banks = [transpose(e_sb[2][:], pair) for pair in range(PAIRS)]
+        e_q.append(quantise(e_grouped[1][:], SIZE, sbuf, "e"))
+        inp_q.append(quantise(inp_grouped[2][:], SIZE, sbuf, "inp"))
+
+        for pair in range(PAIRS):
+            copy_out(e_banks[pair], e_grouped[2], pair, on_vector)
+        vx_q = quantise_vx(0, 0, SIZE)
+        half = SIZE // 2
+        for quarter in range(2):
+            square(2, quarter, first_matmul(inp_q[2], quarter))
+        root(2, 0, half)
+        t_banks = [second_matmul(0, j, vx_q, SIZE) for j in range(TILES)]
+        for quarter in range(2, TILES):
+            square(2, quarter, first_matmul(inp_q[2], quarter))
+        root(2, half, half)
+        e_q.append(quantise(e_grouped[2][:], SIZE, sbuf, "e"))
+        for j in range(TILES):
+            finish(0, j, 0, SIZE, t_banks[j])
+
+        vx_q = quantise_vx(1, 0, SIZE)
+        t_banks = [second_matmul(1, j, vx_q, SIZE) for j in range(TILES)]
+        for j in range(2):
+            finish(1, j, 0, SIZE, t_banks[j])
+        vx_q = quantise_vx(2, 0, half)
+        for j in range(2, TILES):
+            finish(1, j, 0, SIZE, t_banks[j])
+        t_banks = [second_matmul(2, j, vx_q, half) for j in range(TILES)]
+        for j in range(2):
+            finish(2, j, 0, half, t_banks[j])
+        vx_q = quantise_vx(2, half, half)
+        for j in range(2, TILES):
+            finish(2, j, 0, half, t_banks[j])
+        for j in range(TILES):
+            finish(2, j, half, half, second_matmul(2, j, vx_q, half))

@@ -58,11 +58,10 @@ def tile_quantumattentionblock_pb_kernel(tc, xwx, inp, V, x, out):
         load_xwx(0, slice(1, 2))
         load_xwx(0, slice(2, 4))
         load_xwx(1, slice(0, 4))
-        nc.sync.dma_start(out=v_sb[:], in_=V.rearrange("(r p) f -> p r f", p=P))
-        load_inp(0)
         load_xwx(2, slice(0, 4))
-        load_inp(1)
-        load_inp(2)
+        nc.sync.dma_start(out=v_sb[:], in_=V.rearrange("(r p) f -> p r f", p=P))
+        for b in range(IMAGES):
+            load_inp(b)
         for b in range(IMAGES):
             nc.sync.dma_start(out=x_sb[b][:], in_=x[b].rearrange("(p j) d -> p j d", j=TILES))
 
@@ -199,90 +198,94 @@ def tile_quantumattentionblock_pb_kernel(tc, xwx, inp, V, x, out):
         warm = const.tile([P, 1], F32, name="warm")
         nc.scalar.activation(out=warm[:], in_=eps[:], func=ACT.Exp)
 
-        for j in range(TILES):
-            reduce_max(xwx_sb[0][:, j, :], 0, slice(j, j + 1))
-            exp(0, j)
+        for b in range(2):
+            for j in range(TILES):
+                reduce_max(xwx_sb[b][:, j, :], b, slice(j, j + 1))
+                exp(b, j)
 
         v_grouped = grouped_tile(const, "v")
         v_banks = [transpose(v_sb[:], pair) for pair in range(PAIRS)]
         for pair in range(PAIRS):
             copy_out(v_banks[pair], v_grouped, pair, on_scalar)
-        half_1 = fold(xwx_sb[1][:], "fold_256")
-        quarter_1 = fold(half_1[:], "fold_128")
-        reduce_max(quarter_1[:], 1, slice(0, TILES))
-        for j in range(TILES):
-            exp(1, j)
-
-        inp_grouped = [grouped_tile(sbuf, "inp") for b in range(IMAGES)]
-        e_grouped = [grouped_tile(sbuf, "e") for b in range(IMAGES)]
-        inp_banks = [transpose(inp_sb[0][:], pair) for pair in range(PAIRS)]
-        half_2 = fold(xwx_sb[2][:], "fold_256")
-        copy_out(inp_banks[0], inp_grouped[0], 0, on_vector)
-        quarter_2 = fold(half_2[:], "fold_128")
-        copy_out(inp_banks[1], inp_grouped[0], 1, on_vector)
-        reduce_max(quarter_2[:], 2, slice(0, TILES))
+        two_tiles = [slice(0, 2), slice(2, 4)]
+        halves = [fold(xwx_sb[2][:, tiles, :], "fold_256") for tiles in two_tiles]
+        quarters = [fold(halves[i][:], "fold_128") for i in range(2)]
+        for i in range(2):
+            reduce_max(quarters[i][:], 2, two_tiles[i])
         for j in range(TILES):
             exp(2, j)
         nc.scalar.activation(out=warm[:], in_=eps[:], func=ACT.Sqrt)
 
-        e_q = []
-        v_q = quantise(v_grouped[:], SIZE, const, "v")
-        inp_q = [quantise(inp_grouped[0][:], SIZE, sbuf, "inp")]
-        e_banks = [transpose(e_sb[0][:], pair) for pair in range(PAIRS)]
-        inp_banks = [transpose(inp_sb[1][:], pair) for pair in range(PAIRS)]
+        inp_grouped = [grouped_tile(sbuf, "inp") for b in range(IMAGES)]
+        e_grouped = [grouped_tile(sbuf, "e") for b in range(IMAGES)]
+        half = SIZE // 2
 
+        i_banks = [transpose(inp_sb[0][:], pair) for pair in range(PAIRS)]
+        for pair in range(PAIRS):
+            copy_out(i_banks[pair], inp_grouped[0], pair, on_vector)
+        i_banks = [transpose(inp_sb[1][:], pair) for pair in range(PAIRS)]
+        e_banks = [transpose(e_sb[0][:], pair) for pair in range(PAIRS)]
+        v_q = quantise(v_grouped[:], SIZE, const, "v")
+        inp_q = quantise(inp_grouped[0][:], SIZE, sbuf, "inp")
+        u_banks = [first_matmul(inp_q, quarter) for quarter in range(2)]
+        for pair in range(PAIRS):
+            copy_out(i_banks[pair], inp_grouped[1], pair, on_vector)
+        i_banks = [transpose(inp_sb[2][:], pair) for pair in range(PAIRS)]
+        u_banks += [first_matmul(inp_q, quarter) for quarter in range(2, TILES)]
         for quarter in range(TILES):
-            square(0, quarter, first_matmul(inp_q[0], quarter))
+            square(0, quarter, u_banks[quarter])
+
+        copy_out(e_banks[0], e_grouped[0], 0, on_vector)
+        inp_q = quantise(inp_grouped[1][:], SIZE, sbuf, "inp")
+        copy_out(e_banks[1], e_grouped[0], 1, on_vector)
+        square(1, 0, first_matmul(inp_q, 0))
         root(0, 0, SIZE)
-        for pair in range(PAIRS):
-            copy_out(e_banks[pair], e_grouped[0], pair, on_vector)
-        for pair in range(PAIRS):
-            copy_out(inp_banks[pair], inp_grouped[1], pair, on_vector)
         e_banks = [transpose(e_sb[1][:], pair) for pair in range(PAIRS)]
-        e_q.append(quantise(e_grouped[0][:], SIZE, sbuf, "e"))
-        inp_q.append(quantise(inp_grouped[1][:], SIZE, sbuf, "inp"))
-        inp_banks = [transpose(inp_sb[2][:], pair) for pair in range(PAIRS)]
         for b in range(IMAGES):
             nc.vector.reciprocal(out=inverse[b][:], in_=rowsum[b][:])
+        copy_out(i_banks[0], inp_grouped[2], 0, on_vector)
+        e_q = [quantise(e_grouped[0][:], SIZE, sbuf, "e")]
+        copy_out(i_banks[1], inp_grouped[2], 1, on_vector)
+        u_banks = [first_matmul(inp_q, 1)]
 
-        for quarter in range(TILES):
-            square(1, quarter, first_matmul(inp_q[1], quarter))
-        root(1, 0, SIZE)
-        for pair in range(PAIRS):
-            copy_out(e_banks[pair], e_grouped[1], pair, on_vector)
-        for pair in range(PAIRS):
-            copy_out(inp_banks[pair], inp_grouped[2], pair, on_vector)
-        e_banks = [transpose(e_sb[2][:], pair) for pair in range(PAIRS)]
+        e2_banks = [transpose(e_sb[2][:], pair) for pair in range(PAIRS)]
+        u_banks += [first_matmul(inp_q, quarter) for quarter in range(2, TILES)]
+        copy_out(e_banks[0], e_grouped[1], 0, on_vector)
+        inp_q = quantise(inp_grouped[2][:], SIZE, sbuf, "inp")
+        copy_out(e_banks[1], e_grouped[1], 1, on_vector)
+        square(1, 1, u_banks[0])
+        square(1, 2, u_banks[1])
+        root(1, 0, half)
+        u_bank = first_matmul(inp_q, 0)
+        square(1, 3, u_banks[2])
+        square(2, 0, u_bank)
+        root(1, half, half)
+        copy_out(e2_banks[0], e_grouped[2], 0, on_vector)
         e_q.append(quantise(e_grouped[1][:], SIZE, sbuf, "e"))
-        inp_q.append(quantise(inp_grouped[2][:], SIZE, sbuf, "inp"))
 
-        for pair in range(PAIRS):
-            copy_out(e_banks[pair], e_grouped[2], pair, on_vector)
         vx_q = quantise_vx(0, 0, SIZE)
-        half = SIZE // 2
-        for quarter in range(2):
-            square(2, quarter, first_matmul(inp_q[2], quarter))
-        root(2, 0, half)
+        copy_out(e2_banks[1], e_grouped[2], 1, on_vector)
         t_banks = [second_matmul(0, j, vx_q, SIZE) for j in range(TILES)]
-        for quarter in range(2, TILES):
-            square(2, quarter, first_matmul(inp_q[2], quarter))
-        root(2, half, half)
+        u_banks = [first_matmul(inp_q, quarter) for quarter in range(1, 3)]
+        square(2, 1, u_banks[0])
+        square(2, 2, u_banks[1])
+        root(2, 0, half)
         e_q.append(quantise(e_grouped[2][:], SIZE, sbuf, "e"))
-        for j in range(TILES):
+        for j in range(2):
+            finish(0, j, 0, SIZE, t_banks[j])
+        vx_q = quantise_vx(1, 0, half)
+        for j in range(2, TILES):
             finish(0, j, 0, SIZE, t_banks[j])
 
-        vx_q = quantise_vx(1, 0, SIZE)
-        t_banks = [second_matmul(1, j, vx_q, SIZE) for j in range(TILES)]
-        for j in range(2):
-            finish(1, j, 0, SIZE, t_banks[j])
-        vx_q = quantise_vx(2, 0, half)
-        for j in range(2, TILES):
-            finish(1, j, 0, SIZE, t_banks[j])
-        t_banks = [second_matmul(2, j, vx_q, half) for j in range(TILES)]
-        for j in range(2):
-            finish(2, j, 0, half, t_banks[j])
-        vx_q = quantise_vx(2, half, half)
-        for j in range(2, TILES):
-            finish(2, j, 0, half, t_banks[j])
-        for j in range(TILES):
-            finish(2, j, half, half, second_matmul(2, j, vx_q, half))
+        ends = [(1, 0), (1, half), (2, 0), (2, half)]
+        for k in range(len(ends)):
+            b, first = ends[k]
+            t_banks = [second_matmul(b, j, vx_q, half) for j in range(TILES)]
+            if k == 0:
+                square(2, 3, first_matmul(inp_q, 3))
+                root(2, half, half)
+            finish(b, 0, first, half, t_banks[0])
+            if k + 1 < len(ends):
+                vx_q = quantise_vx(ends[k + 1][0], ends[k + 1][1], half)
+            for j in range(1, TILES):
+                finish(b, j, first, half, t_banks[j])

@@ -10,7 +10,6 @@ U8 = mybir.dt.uint8
 FP8X4 = mybir.dt.float8_e4m3fn_x4
 ACT = mybir.ActivationFunctionType
 ALU = mybir.AluOpType
-AXIS = mybir.AxisListType
 
 P = 128
 PACK = 4
@@ -57,8 +56,9 @@ def tile_quantumattentionblock_pb_kernel(tc, xwx, inp, V, x, out):
         load_xwx(0, slice(0, 1))
         load_xwx(0, slice(1, 2))
         load_xwx(0, slice(2, 4))
-        load_xwx(1, slice(0, 4))
-        load_xwx(2, slice(0, 4))
+        for b in range(1, IMAGES):
+            load_xwx(b, slice(0, 2))
+            load_xwx(b, slice(2, 4))
         nc.sync.dma_start(out=v_sb[:], in_=V.rearrange("(r p) f -> p r f", p=P))
         for b in range(IMAGES):
             load_inp(b)
@@ -74,16 +74,17 @@ def tile_quantumattentionblock_pb_kernel(tc, xwx, inp, V, x, out):
             sbuf.tile([P, SIZE, PACK], BF16, name="vx_grouped", align_bytes=64) for b in range(IMAGES)
         ]
 
-        def fold(rows, name):
-            width = rows.shape[2] // 2
-            folded = pieces.tile([P, rows.shape[1], width], BF16, name=name)
-            nc.vector.tensor_tensor(
-                out=folded[:], in0=rows[:, :, 0:width], in1=rows[:, :, width : 2 * width], op=ALU.max
+        def minimum_of_negated(b, j):
+            negated = pieces.tile([P, SIZE], BF16, name="negated")
+            nc.vector.tensor_scalar(
+                out=negated[:],
+                in0=xwx_sb[b][:, j, :],
+                scalar1=-1.0,
+                scalar2=None,
+                op0=ALU.mult,
+                op1=ALU.min,
+                accum_out=negmax[b][:, j : j + 1],
             )
-            return folded
-
-        def reduce_max(rows, b, tiles):
-            nc.vector.tensor_reduce(out=negmax[b][:, tiles], in_=rows, axis=AXIS.X, op=ALU.max, negate=True)
 
         def exp(b, j):
             nc.scalar.activation(
@@ -198,28 +199,20 @@ def tile_quantumattentionblock_pb_kernel(tc, xwx, inp, V, x, out):
         warm = const.tile([P, 1], F32, name="warm")
         nc.scalar.activation(out=warm[:], in_=eps[:], func=ACT.Exp)
 
-        for b in range(2):
+        for b in range(IMAGES):
             for j in range(TILES):
-                reduce_max(xwx_sb[b][:, j, :], b, slice(j, j + 1))
+                minimum_of_negated(b, j)
                 exp(b, j)
-
-        v_grouped = grouped_tile(const, "v")
-        v_banks = [transpose(v_sb[:], pair) for pair in range(PAIRS)]
-        for pair in range(PAIRS):
-            copy_out(v_banks[pair], v_grouped, pair, on_scalar)
-        two_tiles = [slice(0, 2), slice(2, 4)]
-        halves = [fold(xwx_sb[2][:, tiles, :], "fold_256") for tiles in two_tiles]
-        quarters = [fold(halves[i][:], "fold_128") for i in range(2)]
-        for i in range(2):
-            reduce_max(quarters[i][:], 2, two_tiles[i])
-        for j in range(TILES):
-            exp(2, j)
         nc.scalar.activation(out=warm[:], in_=eps[:], func=ACT.Sqrt)
 
+        v_grouped = grouped_tile(const, "v")
         inp_grouped = [grouped_tile(sbuf, "inp") for b in range(IMAGES)]
         e_grouped = [grouped_tile(sbuf, "e") for b in range(IMAGES)]
         half = SIZE // 2
 
+        v_banks = [transpose(v_sb[:], pair) for pair in range(PAIRS)]
+        for pair in range(PAIRS):
+            copy_out(v_banks[pair], v_grouped, pair, on_vector)
         i_banks = [transpose(inp_sb[0][:], pair) for pair in range(PAIRS)]
         for pair in range(PAIRS):
             copy_out(i_banks[pair], inp_grouped[0], pair, on_vector)
@@ -227,50 +220,47 @@ def tile_quantumattentionblock_pb_kernel(tc, xwx, inp, V, x, out):
         e_banks = [transpose(e_sb[0][:], pair) for pair in range(PAIRS)]
         v_q = quantise(v_grouped[:], SIZE, const, "v")
         inp_q = quantise(inp_grouped[0][:], SIZE, sbuf, "inp")
-        u_banks = [first_matmul(inp_q, quarter) for quarter in range(2)]
+        for quarter in range(TILES):
+            square(0, quarter, first_matmul(inp_q, quarter))
+
         for pair in range(PAIRS):
             copy_out(i_banks[pair], inp_grouped[1], pair, on_vector)
-        i_banks = [transpose(inp_sb[2][:], pair) for pair in range(PAIRS)]
-        u_banks += [first_matmul(inp_q, quarter) for quarter in range(2, TILES)]
-        for quarter in range(TILES):
-            square(0, quarter, u_banks[quarter])
-
         copy_out(e_banks[0], e_grouped[0], 0, on_vector)
         inp_q = quantise(inp_grouped[1][:], SIZE, sbuf, "inp")
         copy_out(e_banks[1], e_grouped[0], 1, on_vector)
+        i_banks = [transpose(inp_sb[2][:], 0)]
         square(1, 0, first_matmul(inp_q, 0))
         root(0, 0, SIZE)
-        e_banks = [transpose(e_sb[1][:], pair) for pair in range(PAIRS)]
+        i_banks.append(transpose(inp_sb[2][:], 1))
         for b in range(IMAGES):
             nc.vector.reciprocal(out=inverse[b][:], in_=rowsum[b][:])
-        copy_out(i_banks[0], inp_grouped[2], 0, on_vector)
         e_q = [quantise(e_grouped[0][:], SIZE, sbuf, "e")]
-        copy_out(i_banks[1], inp_grouped[2], 1, on_vector)
+        e_banks = [transpose(e_sb[1][:], pair) for pair in range(PAIRS)]
         u_banks = [first_matmul(inp_q, 1)]
 
+        for pair in range(PAIRS):
+            copy_out(i_banks[pair], inp_grouped[2], pair, on_vector)
+        copy_out(e_banks[0], e_grouped[1], 0, on_vector)
         e2_banks = [transpose(e_sb[2][:], pair) for pair in range(PAIRS)]
         u_banks += [first_matmul(inp_q, quarter) for quarter in range(2, TILES)]
-        copy_out(e_banks[0], e_grouped[1], 0, on_vector)
         inp_q = quantise(inp_grouped[2][:], SIZE, sbuf, "inp")
         copy_out(e_banks[1], e_grouped[1], 1, on_vector)
+        copy_out(e2_banks[0], e_grouped[2], 0, on_vector)
         square(1, 1, u_banks[0])
         square(1, 2, u_banks[1])
+        copy_out(e2_banks[1], e_grouped[2], 1, on_scalar)
         root(1, 0, half)
-        u_bank = first_matmul(inp_q, 0)
         square(1, 3, u_banks[2])
-        square(2, 0, u_bank)
+        square(2, 0, first_matmul(inp_q, 0))
         root(1, half, half)
-        copy_out(e2_banks[0], e_grouped[2], 0, on_vector)
-        e_q.append(quantise(e_grouped[1][:], SIZE, sbuf, "e"))
+        square(2, 1, first_matmul(inp_q, 1))
 
         vx_q = quantise_vx(0, 0, SIZE)
-        copy_out(e2_banks[1], e_grouped[2], 1, on_vector)
-        t_banks = [second_matmul(0, j, vx_q, SIZE) for j in range(TILES)]
-        u_banks = [first_matmul(inp_q, quarter) for quarter in range(1, 3)]
-        square(2, 1, u_banks[0])
-        square(2, 2, u_banks[1])
-        root(2, 0, half)
+        e_q.append(quantise(e_grouped[1][:], SIZE, sbuf, "e"))
         e_q.append(quantise(e_grouped[2][:], SIZE, sbuf, "e"))
+        t_banks = [second_matmul(0, j, vx_q, SIZE) for j in range(TILES)]
+        square(2, 2, first_matmul(inp_q, 2))
+        root(2, 0, half)
         for j in range(2):
             finish(0, j, 0, SIZE, t_banks[j])
         vx_q = quantise_vx(1, 0, half)
@@ -284,8 +274,10 @@ def tile_quantumattentionblock_pb_kernel(tc, xwx, inp, V, x, out):
             if k == 0:
                 square(2, 3, first_matmul(inp_q, 3))
                 root(2, half, half)
-            finish(b, 0, first, half, t_banks[0])
+            passes_before = 2 if k == 2 else 1
+            for j in range(passes_before):
+                finish(b, j, first, half, t_banks[j])
             if k + 1 < len(ends):
                 vx_q = quantise_vx(ends[k + 1][0], ends[k + 1][1], half)
-            for j in range(1, TILES):
+            for j in range(passes_before, TILES):
                 finish(b, j, first, half, t_banks[j])

@@ -29,7 +29,9 @@ def tile_quantumattentionblock_pb_kernel(tc, xwx, inp, V, x, out):
         sbuf = ctx.enter_context(tc.tile_pool(name="sbuf", bufs=IMAGES))
         pieces = ctx.enter_context(tc.tile_pool(name="pieces", bufs=IMAGES + 1))
         psum_vector = ctx.enter_context(tc.psum_pool(name="psum_vector", bufs=4))
-        psum_scalar = ctx.enter_context(tc.psum_pool(name="psum_scalar", bufs=4))
+        psum_scalar = ctx.enter_context(tc.psum_pool(name="psum_scalar", bufs=3))
+        psum_clock = ctx.enter_context(tc.psum_pool(name="psum_clock", bufs=1))
+        unread = psum_clock.tile([P, P], F32, name="unread")
 
         identity = const.tile([P, P], F32, name="identity")
         make_identity(nc, identity[:])
@@ -95,6 +97,10 @@ def tile_quantumattentionblock_pb_kernel(tc, xwx, inp, V, x, out):
                 scale=1.0,
                 accum_out=rowsum[b][:, j : j + 1],
             )
+
+        def keep_clock(count, words):
+            for i in range(count):
+                nc.tensor.matmul(unread[:], lhsT=identity[:], rhs=words, start=True, stop=True)
 
         def transpose(rows, pair):
             row_words = rows.bitcast(F32)
@@ -210,14 +216,18 @@ def tile_quantumattentionblock_pb_kernel(tc, xwx, inp, V, x, out):
         e_grouped = [grouped_tile(sbuf, "e") for b in range(IMAGES)]
         half = SIZE // 2
 
+        keep_clock(3, xwx_sb[2][:, 0, 0 : 2 * P].bitcast(F32))
         v_banks = [transpose(v_sb[:], pair) for pair in range(PAIRS)]
+        keep_clock(1, identity[:])
         for pair in range(PAIRS):
             copy_out(v_banks[pair], v_grouped, pair, on_vector)
         i_banks = [transpose(inp_sb[0][:], pair) for pair in range(PAIRS)]
         for pair in range(PAIRS):
             copy_out(i_banks[pair], inp_grouped[0], pair, on_vector)
+        keep_clock(1, identity[:])
         i_banks = [transpose(inp_sb[1][:], pair) for pair in range(PAIRS)]
         e_banks = [transpose(e_sb[0][:], pair) for pair in range(PAIRS)]
+        keep_clock(2, identity[:])
         v_q = quantise(v_grouped[:], SIZE, const, "v")
         inp_q = quantise(inp_grouped[0][:], SIZE, sbuf, "inp")
         for quarter in range(TILES):
@@ -229,9 +239,11 @@ def tile_quantumattentionblock_pb_kernel(tc, xwx, inp, V, x, out):
         inp_q = quantise(inp_grouped[1][:], SIZE, sbuf, "inp")
         copy_out(e_banks[1], e_grouped[0], 1, on_vector)
         i_banks = [transpose(inp_sb[2][:], 0)]
+        keep_clock(1, identity[:])
         square(1, 0, first_matmul(inp_q, 0))
         root(0, 0, SIZE)
         i_banks.append(transpose(inp_sb[2][:], 1))
+        keep_clock(1, identity[:])
         for b in range(IMAGES):
             nc.vector.reciprocal(out=inverse[b][:], in_=rowsum[b][:])
         e_q = [quantise(e_grouped[0][:], SIZE, sbuf, "e")]
@@ -242,6 +254,7 @@ def tile_quantumattentionblock_pb_kernel(tc, xwx, inp, V, x, out):
             copy_out(i_banks[pair], inp_grouped[2], pair, on_vector)
         copy_out(e_banks[0], e_grouped[1], 0, on_vector)
         e2_banks = [transpose(e_sb[2][:], pair) for pair in range(PAIRS)]
+        keep_clock(1, identity[:])
         u_banks += [first_matmul(inp_q, quarter) for quarter in range(2, TILES)]
         inp_q = quantise(inp_grouped[2][:], SIZE, sbuf, "inp")
         copy_out(e_banks[1], e_grouped[1], 1, on_vector)

@@ -59,9 +59,8 @@ def tile_quantumattentionblock_pb_kernel(tc, xwx, inp, V, x, out):
         load_xwx(0, slice(1, 2))
         load_xwx(0, slice(2, 4))
         for b in range(1, IMAGES):
-            load_xwx(b, slice(0, 2))
-            load_xwx(b, slice(2, 4))
-        nc.sync.dma_start(out=v_sb[:], in_=V.rearrange("(r p) f -> p r f", p=P))
+            load_xwx(b, slice(0, TILES))
+        nc.sync.dma_start(out=v_sb[:], in_=V.rearrange("(p j) f -> p j f", j=TILES))
         for b in range(IMAGES):
             load_inp(b)
         for b in range(IMAGES):
@@ -121,6 +120,15 @@ def tile_quantumattentionblock_pb_kernel(tc, xwx, inp, V, x, out):
             copy(
                 out=words[:, 2 * pair : 2 * pair + 2, :, :],
                 in_=bank[:].rearrange("w tile half r -> w tile r half"),
+            )
+
+        def copy_v_out(bank, pair):
+            words = v_grouped[:].bitcast(F32).rearrange(
+                "w (r tile half) -> w r tile half", tile=TILES, half=2
+            )
+            nc.vector.tensor_copy(
+                out=words[:, :, 2 * pair : 2 * pair + 2, :],
+                in_=bank[:].rearrange("w tile half r -> w r tile half"),
             )
 
         def quantise(grouped, columns, pool, name):
@@ -216,11 +224,11 @@ def tile_quantumattentionblock_pb_kernel(tc, xwx, inp, V, x, out):
         e_grouped = [grouped_tile(sbuf, "e") for b in range(IMAGES)]
         half = SIZE // 2
 
-        keep_clock(3, xwx_sb[2][:, 0, 0 : 2 * P].bitcast(F32))
+        keep_clock(3, xwx_sb[1][:, 0, 0 : 2 * P].bitcast(F32))
         v_banks = [transpose(v_sb[:], pair) for pair in range(PAIRS)]
         keep_clock(1, identity[:])
         for pair in range(PAIRS):
-            copy_out(v_banks[pair], v_grouped, pair, on_vector)
+            copy_v_out(v_banks[pair], pair)
         i_banks = [transpose(inp_sb[0][:], pair) for pair in range(PAIRS)]
         for pair in range(PAIRS):
             copy_out(i_banks[pair], inp_grouped[0], pair, on_vector)

from contextlib import ExitStack

import concourse.mybir as mybir
from concourse.masks import make_identity

F32 = mybir.dt.float32
BF16 = mybir.dt.bfloat16
U32 = mybir.dt.uint32
U8 = mybir.dt.uint8
FP8X4 = mybir.dt.float8_e4m3fn_x4
ACT = mybir.ActivationFunctionType
ALU = mybir.AluOpType

P = 128
PACK = 4
IMAGES = 3
SIZE = 512
TILES = SIZE // P
PAIRS = TILES // 2
EPS = 1e-8

FLOPS = 2 * 2 * IMAGES * SIZE * SIZE * SIZE


def tile_quantumattentionblock_pb_kernel(tc, xwx, inp, V, x, out):
    nc = tc.nc
    with ExitStack() as ctx:
        const = ctx.enter_context(tc.tile_pool(name="const", bufs=1))
        sbuf = ctx.enter_context(tc.tile_pool(name="sbuf", bufs=IMAGES))
        pieces = ctx.enter_context(tc.tile_pool(name="pieces", bufs=IMAGES + 1))
        psum_vector = ctx.enter_context(tc.psum_pool(name="psum_vector", bufs=4))
        psum_scalar = ctx.enter_context(tc.psum_pool(name="psum_scalar", bufs=3))
        psum_clock = ctx.enter_context(tc.psum_pool(name="psum_clock", bufs=1))
        unread = psum_clock.tile([P, P], F32, name="unread")

        identity = const.tile([P, P], F32, name="identity")
        make_identity(nc, identity[:])
        eps = const.tile([P, 1], F32, name="eps")
        nc.vector.memset(eps[:], EPS)

        ctx.enter_context(tc.manual_schedule())

        xwx_sb = [sbuf.tile([P, TILES, SIZE], BF16, name="xwx_sb") for b in range(IMAGES)]
        inp_sb = [sbuf.tile([P, TILES, SIZE], BF16, name="inp_sb") for b in range(IMAGES)]
        x_sb = [sbuf.tile([P, TILES, SIZE], BF16, name="x_sb") for b in range(IMAGES)]
        v_sb = const.tile([P, TILES, SIZE], BF16, name="v_sb")

        def load_xwx(b, tiles):
            rows = xwx[b].rearrange("(p j) n -> p j n", j=TILES)
            nc.sync.dma_start(out=xwx_sb[b][:, tiles, :], in_=rows[:, tiles, :])

        def load_inp(b):
            nc.sync.dma_start(
                out=inp_sb[b][:].rearrange("p (half odd) f -> p half odd f", odd=2),
                in_=inp[b].rearrange("(half p odd) f -> p half odd f", half=2, odd=2),
            )

        load_xwx(0, slice(0, 1))
        load_xwx(0, slice(1, 2))
        load_xwx(0, slice(2, 4))
        for b in range(1, IMAGES):
            load_xwx(b, slice(0, TILES))
        nc.sync.dma_start(out=v_sb[:], in_=V.rearrange("(p j) f -> p j f", j=TILES))
        for b in range(IMAGES):
            load_inp(b)
        for b in range(IMAGES):
            nc.sync.dma_start(out=x_sb[b][:], in_=x[b].rearrange("(p j) d -> p j d", j=TILES))

        e_sb = [sbuf.tile([P, TILES, SIZE], BF16, name="e_sb") for b in range(IMAGES)]
        negmax = [sbuf.tile([P, TILES], F32, name="negmax") for b in range(IMAGES)]
        rowsum = [sbuf.tile([P, TILES], F32, name="rowsum") for b in range(IMAGES)]
        inverse = [sbuf.tile([P, TILES], F32, name="inverse") for b in range(IMAGES)]
        squares = [sbuf.tile([P, SIZE, TILES], F32, name="squares") for b in range(IMAGES)]
        vx_grouped = [
            sbuf.tile([P, SIZE, PACK], BF16, name="vx_grouped", align_bytes=64) for b in range(IMAGES)
        ]

        def minimum_of_negated(b, j):
            negated = pieces.tile([P, SIZE], BF16, name="negated")
            nc.vector.tensor_scalar(
                out=negated[:],
                in0=xwx_sb[b][:, j, :],
                scalar1=-1.0,
                scalar2=None,
                op0=ALU.mult,
                op1=ALU.min,
                accum_out=negmax[b][:, j : j + 1],
            )

        def exp(b, j):
            nc.scalar.activation(
                out=e_sb[b][:, j, :],
                in_=xwx_sb[b][:, j, :],
                func=ACT.Exp,
                bias=negmax[b][:, j : j + 1],
                scale=1.0,
                accum_out=rowsum[b][:, j : j + 1],
            )

        def keep_clock(count, words):
            for i in range(count):
                nc.tensor.matmul(unread[:], lhsT=identity[:], rhs=words, start=True, stop=True)

        def transpose(rows, pair):
            row_words = rows.bitcast(F32)
            bank = psum_vector.tile([P, 2, 2, P], F32, name="transposed", tag="for_vector")
            for tile_in_pair in range(2):
                for half in range(2):
                    nc.tensor.transpose(
                        bank[:, tile_in_pair, half, :],
                        row_words[:, 2 * pair + tile_in_pair, half * P : (half + 1) * P],
                        identity[:],
                    )
            return bank

        def copy_out(bank, grouped, pair, copy):
            words = grouped[:].bitcast(F32).rearrange(
                "w (tile r half) -> w tile r half", tile=TILES, half=2
            )
            copy(
                out=words[:, 2 * pair : 2 * pair + 2, :, :],
                in_=bank[:].rearrange("w tile half r -> w tile r half"),
            )

        def copy_v_out(bank, pair):
            words = v_grouped[:].bitcast(F32).rearrange(
                "w (r tile half) -> w r tile half", tile=TILES, half=2
            )
            nc.vector.tensor_copy(
                out=words[:, :, 2 * pair : 2 * pair + 2, :],
                in_=bank[:].rearrange("w tile half r -> w r tile half"),
            )

        def quantise(grouped, columns, pool, name):
            codes = pool.tile([P, columns], U32, name=name + "_codes", align_bytes=64)
            scales = pool.tile([P, columns], U8, name=name + "_scales", align_bytes=64)
            nc.vector.quantize_mx(out=codes[:].bitcast(FP8X4), scales=scales[:], in_=grouped)
            return codes, scales

        def first_matmul(inp_q, quarter):
            inp_codes, inp_scales = inp_q
            v_codes, v_scales = v_q
            features = slice(quarter * P, (quarter + 1) * P)
            u_bank = psum_scalar.tile([P, TILES, P], F32, name="u_bank")
            for m in range(TILES):
                patches = slice(m * P, (m + 1) * P)
                nc.tensor.matmul_mx(
                    out=u_bank[:, m, :],
                    lhsT=inp_codes[:, patches].bitcast(FP8X4),
                    lhsT_scale=inp_scales[:, patches],
                    rhs=v_codes[:, features].bitcast(FP8X4),
                    rhs_scale=v_scales[:, features],
                    start=True,
                    stop=True,
                )
            return u_bank

        def square(b, quarter, u_bank):
            nc.scalar.activation(
                out=squares[b][:, quarter * P : (quarter + 1) * P, :],
                in_=u_bank[:].rearrange("p m d -> p d m"),
                func=ACT.Square,
            )

        def root(b, first, width):
            nc.scalar.activation(
                out=vx_grouped[b][:, first : first + width, :],
                in_=squares[b][:, first : first + width, :],
                func=ACT.Sqrt,
                bias=eps[:],
                scale=1.0,
            )

        def quantise_vx(b, first, width):
            some = vx_grouped[b][:, first : first + width, :]
            return quantise(some.rearrange("p d m -> p (d m)"), width, pieces, "vx")

        def second_matmul(b, j, vx_q, width):
            e_codes, e_scales = e_q[b]
            vx_codes, vx_scales = vx_q
            queries = slice(j * P, (j + 1) * P)
            t_bank = psum_vector.tile([P, width], F32, name="t_bank", tag="for_vector")
            nc.tensor.matmul_mx(
                out=t_bank[:],
                lhsT=e_codes[:, queries].bitcast(FP8X4),
                lhsT_scale=e_scales[:, queries],
                rhs=vx_codes[:].bitcast(FP8X4),
                rhs_scale=vx_scales[:],
                start=True,
                stop=True,
            )
            return t_bank

        def finish(b, j, first, width, t_bank):
            out_sb = pieces.tile([P, width], F32, name="out_sb", bufs=2 * TILES)
            nc.vector.scalar_tensor_tensor(
                out=out_sb[:],
                in0=t_bank[:],
                scalar=inverse[b][:, j : j + 1],
                in1=x_sb[b][:, j, first : first + width],
                op0=ALU.mult,
                op1=ALU.add,
            )
            out_rows = out[b].rearrange("(p j) d -> p j d", j=TILES)
            nc.sync.dma_start(out=out_rows[:, j, first : first + width], in_=out_sb[:])

        def grouped_tile(pool, name):
            return pool.tile([P, PACK * SIZE], BF16, name=name + "_grouped", align_bytes=64)

        on_vector = nc.vector.tensor_copy
        on_scalar = nc.scalar.copy

        warm = const.tile([P, 1], F32, name="warm")
        nc.scalar.activation(out=warm[:], in_=eps[:], func=ACT.Exp)

        for b in range(IMAGES):
            for j in range(TILES):
                minimum_of_negated(b, j)
                exp(b, j)
        nc.scalar.activation(out=warm[:], in_=eps[:], func=ACT.Sqrt)

        v_grouped = grouped_tile(const, "v")
        inp_grouped = [grouped_tile(sbuf, "inp") for b in range(IMAGES)]
        e_grouped = [grouped_tile(sbuf, "e") for b in range(IMAGES)]
        half = SIZE // 2

        keep_clock(3, xwx_sb[1][:, 0, 0 : 2 * P].bitcast(F32))
        v_banks = [transpose(v_sb[:], pair) for pair in range(PAIRS)]
        keep_clock(1, identity[:])
        for pair in range(PAIRS):
            copy_v_out(v_banks[pair], pair)
        i_banks = [transpose(inp_sb[0][:], pair) for pair in range(PAIRS)]
        for pair in range(PAIRS):
            copy_out(i_banks[pair], inp_grouped[0], pair, on_vector)
        keep_clock(1, identity[:])
        i_banks = [transpose(inp_sb[1][:], pair) for pair in range(PAIRS)]
        e_banks = [transpose(e_sb[0][:], pair) for pair in range(PAIRS)]
        keep_clock(2, identity[:])
        v_q = quantise(v_grouped[:], SIZE, const, "v")
        inp_q = quantise(inp_grouped[0][:], SIZE, sbuf, "inp")
        for quarter in range(TILES):
            square(0, quarter, first_matmul(inp_q, quarter))

        for pair in range(PAIRS):
            copy_out(i_banks[pair], inp_grouped[1], pair, on_vector)
        copy_out(e_banks[0], e_grouped[0], 0, on_vector)
        inp_q = quantise(inp_grouped[1][:], SIZE, sbuf, "inp")
        copy_out(e_banks[1], e_grouped[0], 1, on_vector)
        i_banks = [transpose(inp_sb[2][:], 0)]
        keep_clock(1, identity[:])
        square(1, 0, first_matmul(inp_q, 0))
        root(0, 0, SIZE)
        i_banks.append(transpose(inp_sb[2][:], 1))
        keep_clock(1, identity[:])
        for b in range(IMAGES):
            nc.vector.reciprocal(out=inverse[b][:], in_=rowsum[b][:])
        e_q = [quantise(e_grouped[0][:], SIZE, sbuf, "e")]
        e_banks = [transpose(e_sb[1][:], pair) for pair in range(PAIRS)]
        u_banks = [first_matmul(inp_q, 1)]

        for pair in range(PAIRS):
            copy_out(i_banks[pair], inp_grouped[2], pair, on_vector)
        copy_out(e_banks[0], e_grouped[1], 0, on_vector)
        e2_banks = [transpose(e_sb[2][:], pair) for pair in range(PAIRS)]
        keep_clock(1, identity[:])
        u_banks += [first_matmul(inp_q, quarter) for quarter in range(2, TILES)]
        inp_q = quantise(inp_grouped[2][:], SIZE, sbuf, "inp")
        copy_out(e_banks[1], e_grouped[1], 1, on_vector)
        copy_out(e2_banks[0], e_grouped[2], 0, on_vector)
        square(1, 1, u_banks[0])
        square(1, 2, u_banks[1])
        copy_out(e2_banks[1], e_grouped[2], 1, on_scalar)
        root(1, 0, half)
        square(1, 3, u_banks[2])
        square(2, 0, first_matmul(inp_q, 0))
        root(1, half, half)
        square(2, 1, first_matmul(inp_q, 1))

        vx_q = quantise_vx(0, 0, SIZE)
        e_q.append(quantise(e_grouped[1][:], SIZE, sbuf, "e"))
        e_q.append(quantise(e_grouped[2][:], SIZE, sbuf, "e"))
        t_banks = [second_matmul(0, j, vx_q, SIZE) for j in range(TILES)]
        square(2, 2, first_matmul(inp_q, 2))
        root(2, 0, half)
        for j in range(2):
            finish(0, j, 0, SIZE, t_banks[j])
        vx_q = quantise_vx(1, 0, half)
        for j in range(2, TILES):
            finish(0, j, 0, SIZE, t_banks[j])

        ends = [(1, 0), (1, half), (2, 0), (2, half)]
        for k in range(len(ends)):
            b, first = ends[k]
            t_banks = [second_matmul(b, j, vx_q, half) for j in range(TILES)]
            if k == 0:
                square(2, 3, first_matmul(inp_q, 3))
                root(2, half, half)
            passes_before = 2 if k == 2 else 1
            for j in range(passes_before):
                finish(b, j, first, half, t_banks[j])
            if k + 1 < len(ends):
                vx_q = quantise_vx(ends[k + 1][0], ends[k + 1][1], half)
            for j in range(passes_before, TILES):
                finish(b, j, first, half, t_banks[j])
